import numpy as np
import ml_dtypes


def mxq(x, axis, fmt="e4m3"):
    dtype, down = {"e4m3": (ml_dtypes.float8_e4m3fn, 7), "e5m2": (ml_dtypes.float8_e5m2, 14)}[fmt]
    v = np.moveaxis(np.asarray(x, np.float32).astype(ml_dtypes.bfloat16).astype(np.float64), axis, -1)
    blocks = v.reshape(v.shape[:-1] + (-1, 32))
    amax = np.abs(blocks).max(-1, keepdims=True)
    byte = np.maximum(np.where(amax > 0, np.frexp(amax)[1] - 1 + 127, 0) - down, 1)
    scale = np.exp2(byte - 127.0)
    codes = (blocks / scale).astype(np.float32).astype(dtype).astype(np.float64)
    return np.moveaxis((codes * scale).reshape(v.shape), -1, axis)


WIDE = False


def mx_kscale(k):
    if not WIDE:
        return np.ones(k)
    levels = np.array([10, -10, 5, -5, 0])
    if k % 512:
        return np.exp2(np.random.permutation(np.resize(levels, k // 32))).repeat(32)
    a = np.empty((k // 512, 16))
    for p in range(k // 512):
        a[p, :8] = np.random.permutation(np.resize(levels, 8))
        for g in range(8):
            far = levels[np.abs(levels - a[p, g]) >= 10]
            a[p, g + 8] = far[np.random.randint(len(far))]
    return np.exp2(a.ravel()).repeat(32)


BF16 = ml_dtypes.bfloat16


def bf(x):
    return np.asarray(x, np.float32).astype(BF16)


def f64(x):
    return np.asarray(x).astype(np.float64)


B, GH, GW, E, H, DH = 128, 7, 7, 512, 8, 64
S = GH * GW
N = H * DH
BASE = 100.0


def rope_half(xh, ang):
    x1, x2 = xh[..., 0::2], xh[..., 1::2]
    cos = np.cos(ang)[None, :, None, :]
    sin = np.sin(ang)[None, :, None, :]
    o1 = x1 * cos - x2 * sin
    o2 = x1 * sin + x2 * cos
    return np.stack([o1, o2], axis=-1).reshape(xh.shape)


def rope_2d(t):
    dh = DH // 2
    rows = f64(np.repeat(np.arange(GH), GW))
    cols = f64(np.tile(np.arange(GW), GH))
    inv_freq = BASE ** (-f64(np.arange(0, dh, 2)) / dh)
    ang_r = rows[:, None] * inv_freq[None, :]
    ang_c = cols[:, None] * inv_freq[None, :]
    tr = rope_half(t[..., :dh], ang_r)
    tc = rope_half(t[..., dh:], ang_c)
    return np.concatenate([tr, tc], axis=-1)


def draw0():
    s = mx_kscale(E)
    w = 1.0 / np.sqrt(E)
    return {"x": bf(np.random.standard_normal((B, S, E)) * s),
            "Wq": bf(np.random.standard_normal((E, N)) * w / s[:, None]),
            "bq": bf(np.random.standard_normal(N) * 0.3),
            "Wk": bf(np.random.standard_normal((E, N)) * w / s[:, None]),
            "bk": bf(np.random.standard_normal(N) * 0.3)}


def core(x, Wq, bq, Wk, bk):
    xq = mxq(f64(x), 2, "e4m3")
    q = ((xq @ mxq(f64(Wq), 0, "e4m3")) + f64(bq)).reshape(B, S, H, DH)
    k = ((xq @ mxq(f64(Wk), 0, "e4m3")) + f64(bk)).reshape(B, S, H, DH)
    return rope_2d(q), rope_2d(k)


def e4m3fn_bytes(y):
    return np.clip(np.asarray(y, np.float64), -448.0, 448.0).astype(np.float32).astype(ml_dtypes.float8_e4m3fn).view(np.uint8)


def e4m3fn_values(b):
    return np.asarray(b, np.uint8).view(ml_dtypes.float8_e4m3fn).astype(np.float64)


def setup_inputs():
    d = draw0()
    x0 = np.asarray(d['x']).astype(np.float64)
    s = (np.max(np.abs(x0), axis=(0, 1), keepdims=True) / 448.0).astype(np.float32)
    out = {}
    for k, v in d.items():
        if k == 'x':
            out['x_bytes'] = e4m3fn_bytes(x0 / s.astype(np.float64))
            out['x_scale'] = s
        else:
            out[k] = v
    return out


def reference(x_bytes, x_scale, Wq, bq, Wk, bk):
    return core(e4m3fn_values(x_bytes) * x_scale.astype(np.float64), Wq, bq, Wk, bk)

@@ -1,0 +1,396 @@
+from contextlib import ExitStack
+
+import concourse.mybir as mybir
+from concourse.masks import make_identity
+
+F32 = mybir.dt.float32
+BF16 = mybir.dt.bfloat16
+U32 = mybir.dt.uint32
+U8 = mybir.dt.uint8
+I32 = mybir.dt.int32
+FP8 = mybir.dt.float8_e4m3fn
+FP8X4 = mybir.dt.float8_e4m3fn_x4
+ALU = mybir.AluOpType
+ACT = mybir.ActivationFunctionType
+
+P = 128
+GRID = 7
+E = 512
+HEADS = 8
+NFREQ = 16
+FLOPS = 2 * 128 * 49 * 512 * 1024
+
+SPLIT = ((0, 4), (4, 3))
+SCALAR_SHARE = 1
+GP_TAN = True
+LAG = 2
+MANUAL_PE = False
+MAX_JOBS = 3
+
+
+def tile_attention_pa_kernel(tc, x_bytes, x_scale, Wq, bq, Wk, bk, out_0, out_1):
+    nc = tc.nc
+    grids = [(r0, nr, c0, ncol) for (r0, nr) in SPLIT for (c0, ncol) in SPLIT]
+    outs = (
+        out_0.rearrange("b s h d -> b s (h d)"),
+        out_1.rearrange("b s h d -> b s (h d)"),
+    )
+
+    with ExitStack() as ctx:
+        const = ctx.enter_context(tc.tile_pool(name="const", bufs=1))
+        wprep = ctx.enter_context(tc.tile_pool(name="wprep", bufs=2))
+        xstream = ctx.enter_context(tc.tile_pool(name="xstream", bufs=3))
+        terms = ctx.enter_context(tc.tile_pool(name="terms", bufs=4))
+        rot = ctx.enter_context(tc.tile_pool(name="rot", bufs=32))
+        stage_pool = ctx.enter_context(tc.tile_pool(name="stage", bufs=8))
+        mm = ctx.enter_context(tc.psum_pool(name="mm", bufs=2))
+        tp = ctx.enter_context(tc.psum_pool(name="tp", bufs=3))
+        if MANUAL_PE:
+            ctx.enter_context(tc.manual_schedule(engines={mybir.EngineType.PE}))
+
+        ident = const.tile([P, P], F32, name="ident")
+        nc.vector.memset(ident[:], 0.0)
+        make_identity(nc, ident[:], nomemset=True)
+        brow = const.tile([P, E], BF16, name="brow")
+        nc.vector.memset(brow[:], 0.0)
+
+        sc4 = const.tile([P, 4 * E], F32, name="sc4")
+        nc.sync.dma_start(out=sc4[:, 0:E], in_=x_scale.rearrange("a b k -> (a b k)").partition_broadcast(P))
+        xv = x_bytes.rearrange("b (r c) k -> b r (c k)", r=GRID, c=GRID)
+        xb = []
+        xcodes = []
+        xscales = []
+        for g, (r0, nr, c0, ncol) in enumerate(grids):
+            xb_g = const.tile([P, nr, ncol * E], U8, name="xb%d" % g)
+            xc_g = const.tile([P, nr * ncol * P], U32, name="xc%d" % g, align_bytes=64)
+            xs_g = const.tile([P, nr * ncol * P], U8, name="xs%d" % g, align_bytes=64)
+            xb.append(xb_g)
+            xcodes.append(xc_g)
+            xscales.append(xs_g)
+        wraws = []
+        btabs = []
+        for qk in range(2):
+            wraw = wprep.tile([P, 4, E], BF16, tag="wraw")
+            wraws.append(wraw)
+            btab = const.tile([P, E], BF16, name="btab%d" % qk)
+            btabs.append(btab)
+
+        def load_x(g, rows):
+            r0, nr, c0, ncol = grids[g]
+            nc.sync.dma_start(out=xb[g][:, rows[0]:rows[1], :],
+                              in_=xv[:, r0 + rows[0]:r0 + rows[1], c0 * E:(c0 + ncol) * E])
+
+        load_x(0, (0, 1))
+        nc.sync.dma_start(out=wraws[0][:], in_=Wq.rearrange("(p t) n -> p t n", t=4))
+        load_x(0, (1, 2))
+        nc.sync.dma_start(out=brow[0:1, :], in_=bq.rearrange("(o n) -> o n", o=1))
+        nc.sync.dma_start(out=brow[1:2, :], in_=bk.rearrange("(o n) -> o n", o=1))
+        load_x(0, (2, 4))
+        nc.sync.dma_start(out=wraws[1][:], in_=Wk.rearrange("(p t) n -> p t n", t=4))
+        nc.sync.dma_start(out=btabs[0][:], in_=bq.partition_broadcast(P))
+        nc.sync.dma_start(out=btabs[1][:], in_=bk.partition_broadcast(P))
+        for g in range(1, len(grids)):
+            load_x(g, (0, grids[g][1]))
+
+        pidx = const.tile([P, 1], I32, name="pidx")
+        nc.gpsimd.iota(pidx[:], pattern=[[0, 1]], base=0, channel_multiplier=1)
+        posi = const.tile([P, GRID], I32, name="posi")
+        nc.gpsimd.iota(posi[:], pattern=[[1, GRID]], base=0, channel_multiplier=0)
+        bits = const.tile([P, 4], I32, name="bits")
+        fac = const.tile([P, 4], F32, name="fac")
+        for i in range(4):
+            nc.vector.tensor_scalar(out=bits[:, i:i + 1], in0=pidx[:], scalar1=i, scalar2=1,
+                                    op0=ALU.logical_shift_right, op1=ALU.bitwise_and)
+        for i in range(4):
+            g_i = 100.0 ** (-(2.0 ** i) / 16.0)
+            nc.vector.tensor_scalar(out=fac[:, i:i + 1], in0=bits[:, i:i + 1], scalar1=g_i - 1.0, scalar2=1.0,
+                                    op0=ALU.mult, op1=ALU.add)
+        f01 = const.tile([P, 1], F32, name="f01")
+        f23 = const.tile([P, 1], F32, name="f23")
+        freq = const.tile([P, 1], F32, name="freq")
+        nc.vector.tensor_tensor(out=f01[:], in0=fac[:, 0:1], in1=fac[:, 1:2], op=ALU.mult)
+        nc.vector.tensor_tensor(out=f23[:], in0=fac[:, 2:3], in1=fac[:, 3:4], op=ALU.mult)
+        nc.vector.tensor_tensor(out=freq[:], in0=f01[:], in1=f23[:], op=ALU.mult)
+        theta = const.tile([P, GRID], F32, name="theta")
+        nc.vector.tensor_scalar(out=theta[:], in0=posi[:], scalar1=freq[:, 0:1], scalar2=None, op0=ALU.mult)
+        s8 = const.tile([P, GRID], F32, name="s8")
+        s4 = const.tile([P, GRID], F32, name="s4")
+        nc.scalar.activation(out=s8[:], in_=theta[:], func=ACT.Sin, scale=0.125)
+        nc.scalar.activation(out=s4[:], in_=theta[:], func=ACT.Sin, scale=0.25)
+
+        def one_minus_twice_square(name, s_ap):
+            sq = const.tile([P, GRID], F32, name=name + "_sq")
+            c_t = const.tile([P, GRID], F32, name=name)
+            nc.vector.tensor_tensor(out=sq[:], in0=s_ap, in1=s_ap, op=ALU.mult)
+            nc.vector.tensor_scalar(out=c_t[:], in0=sq[:], scalar1=-2.0, scalar2=1.0, op0=ALU.mult, op1=ALU.add)
+            return c_t
+
+        c4 = one_minus_twice_square("c4", s8[:])
+        s2 = const.tile([P, GRID], F32, name="s2")
+        nc.vector.scalar_tensor_tensor(out=s2[:], in0=s4[:], scalar=2.0, in1=c4[:], op0=ALU.mult, op1=ALU.mult)
+        c2 = one_minus_twice_square("c2", s4[:])
+        sn = const.tile([P, GRID], F32, name="sn")
+        nc.vector.scalar_tensor_tensor(out=sn[:], in0=s2[:], scalar=2.0, in1=c2[:], op0=ALU.mult, op1=ALU.mult)
+        cs = one_minus_twice_square("cs", s2[:])
+        nsn = const.tile([P, GRID], F32, name="nsn")
+        nc.vector.tensor_scalar(out=nsn[:], in0=sn[:], scalar1=-1.0, scalar2=None, op0=ALU.mult)
+        tan = const.tile([P, GRID], F32, name="tan")
+        if GP_TAN:
+            rcs = const.tile([P, GRID], F32, name="rcs")
+            nc.vector.reciprocal(out=rcs[:], in_=cs[:])
+            nc.vector.tensor_tensor(out=tan[:], in0=sn[:], in1=rcs[:], op=ALU.mult)
+
+        bias_e = const.tile([P, 4, GRID], F32, name="bias_e")
+        bias_o = const.tile([P, 4, GRID], F32, name="bias_o")
+        bias_t = const.tile([P, 4, GRID], F32, name="bias_t")
+
+        def bias_prep():
+            bperm = const.tile([P, E], F32, name="bperm")
+            bsrc = brow[:].rearrange("p (h a j e) -> p a e h j", h=HEADS, a=2, j=NFREQ, e=2)
+            bdst = bperm[:].rearrange("p (a e h j) -> p a e h j", a=2, e=2, h=HEADS, j=NFREQ)
+            for a in range(2):
+                nc.gpsimd.tensor_copy(out=bdst[:, a], in_=bsrc[:, a])
+            bps = tp.tile([P, E], F32, tag="tp")
+            for blk in range(4):
+                nc.tensor.transpose(out=bps[:, blk * P:(blk + 1) * P], in_=bperm[:, blk * P:(blk + 1) * P],
+                                    identity=ident[:])
+            bc = const.tile([P, 2, 2, 2], F32, name="bc")
+            nc.scalar.copy(out=bc[:], in_=bps[:].rearrange("p (a e n) -> p e n a", a=2, e=2)[:, :, 0:2, :])
+            shape = [P, 4, GRID]
+            b_a = bc[:, 0].rearrange("p q a -> p (q a)").unsqueeze(2).to_broadcast(shape)
+            b_b = bc[:, 1].rearrange("p q a -> p (q a)").unsqueeze(2).to_broadcast(shape)
+            cs_b = cs[:].unsqueeze(1).to_broadcast(shape)
+            sn_b = sn[:].unsqueeze(1).to_broadcast(shape)
+            m1 = const.tile(shape, F32, name="m1")
+            m2 = const.tile(shape, F32, name="m2")
+            m3 = const.tile(shape, F32, name="m3")
+            m4 = const.tile(shape, F32, name="m4")
+            nc.gpsimd.tensor_tensor(out=m1[:], in0=cs_b, in1=b_a, op=ALU.mult)
+            nc.gpsimd.tensor_tensor(out=m2[:], in0=sn_b, in1=b_b, op=ALU.mult)
+            nc.gpsimd.tensor_tensor(out=m3[:], in0=sn_b, in1=b_a, op=ALU.mult)
+            nc.gpsimd.tensor_tensor(out=m4[:], in0=cs_b, in1=b_b, op=ALU.mult)
+            nc.gpsimd.tensor_tensor(out=bias_e[:], in0=m1[:], in1=m2[:], op=ALU.subtract)
+            nc.gpsimd.tensor_tensor(out=bias_o[:], in0=m3[:], in1=m4[:], op=ALU.add)
+            if GP_TAN:
+                m5 = const.tile(shape, F32, name="m5")
+                nc.gpsimd.tensor_tensor(out=m5[:], in0=tan[:].unsqueeze(1).to_broadcast(shape), in1=bias_e[:],
+                                        op=ALU.mult)
+                nc.gpsimd.tensor_tensor(out=bias_t[:], in0=bias_o[:], in1=m5[:], op=ALU.subtract)
+
+        def scale_table():
+            nc.scalar.copy(out=sc4[:, E:2 * E], in_=sc4[:, 0:E])
+            nc.scalar.copy(out=sc4[:, 2 * E:4 * E], in_=sc4[:, 0:2 * E])
+
+        wcodes = []
+        wscales = []
+
+        def w_prep(qk):
+            wgrp = wprep.tile([P, E, 4], BF16, tag="wgrp", align_bytes=64)
+            src = wraws[qk][:].rearrange("p t (h a j e) -> p a e h j t", h=HEADS, a=2, j=NFREQ, e=2)
+            dst = wgrp[:].rearrange("p (a e h j) t -> p a e h j t", a=2, e=2, h=HEADS, j=NFREQ)
+            for a in range(2):
+                for e in range(2):
+                    nc.scalar.copy(out=dst[:, a, e], in_=src[:, a, e])
+            wc = const.tile([P, E], U32, name="wc%d" % qk, align_bytes=64)
+            ws = const.tile([P, E], U8, name="ws%d" % qk, align_bytes=64)
+            nc.vector.quantize_mx(out=wc[:].bitcast(FP8X4), scales=ws[:], in_=wgrp[:].rearrange("p c t -> p (c t)"))
+            wcodes.append(wc)
+            wscales.append(ws)
+
+        def x_open(g, ri):
+            ncol = grids[g][3]
+            xs = xstream.tile([P, 4 * E], BF16, tag="xs", align_bytes=64)
+            if g == 0 and ri == 0:
+                for ci in range(ncol):
+                    nc.vector.tensor_tensor(out=xs[:, ci * E:(ci + 1) * E],
+                                            in0=xb[g][:, ri, ci * E:(ci + 1) * E].bitcast(FP8), in1=sc4[:, 0:E],
+                                            op=ALU.mult)
+            else:
+                nc.vector.tensor_tensor(out=xs[:, :ncol * E], in0=xb[g][:, ri, :].bitcast(FP8),
+                                        in1=sc4[:, :ncol * E], op=ALU.mult)
+            grp = xstream.tile([P, 4 * E], BF16, tag="grp", align_bytes=64)
+            return [("x", g, ri, first, xs, grp) for first in range(0, ncol, 2)]
+
+        def x_bank(g, ri, first, xs, grp):
+            ncol = grids[g][3]
+            words = xs[:].bitcast(F32)
+            gwords = grp[:].bitcast(F32)
+            n2 = min(2, ncol - first)
+            xt = tp.tile([P, E], F32, tag="tp")
+            for s2 in range(n2):
+                ci = first + s2
+                for u in range(2):
+                    nc.tensor.transpose(out=xt[:, (s2 * 2 + u) * P:(s2 * 2 + u + 1) * P],
+                                        in_=words[:, ci * 256 + u:(ci + 1) * 256:2], identity=ident[:])
+            nc.scalar.copy(
+                out=gwords[:, first * 256:(first + n2) * 256].rearrange("p (s b u) -> p s b u", s=n2, u=2),
+                in_=xt[:, :n2 * 256].rearrange("p (s u b) -> p s b u", s=n2, u=2))
+            if first + n2 == ncol:
+                col = ri * ncol * P
+                off = 0
+                for width in ((2048,) if ncol == 4 else (1024, 512)):
+                    nc.vector.quantize_mx(out=xcodes[g][:, col:col + width // 4].bitcast(FP8X4),
+                                          scales=xscales[g][:, col:col + width // 4],
+                                          in_=grp[:, off:off + width])
+                    col += width // 4
+                    off += width
+
+        def unit(g, qk, a, idx, o_tiles):
+            r0, nr, c0, ncol = grids[g]
+            if a == 0:
+                pos = r0 + idx
+                n = ncol
+                base = idx * ncol * P
+                chunks = [(0, base, 512)] if ncol == 4 else [(0, base, 256), (256, base + 256, 128)]
+            else:
+                pos = c0 + idx
+                n = nr
+                chunks = [(ri * P, (ri * ncol + idx) * P, P) for ri in range(nr)]
+            bank_a = mm.tile([P, E], F32, tag="A")
+            bank_b = mm.tile([P, E], F32, tag="B", bufs=3)
+            for e, bank in ((0, bank_a), (1, bank_b)):
+                ft = a * 2 + e
+                for dst, src, width in chunks:
+                    nc.tensor.matmul_mx(out=bank[:, dst:dst + width],
+                                        lhsT=wcodes[qk][:, ft * P:(ft + 1) * P].bitcast(FP8X4),
+                                        lhsT_scale=wscales[qk][:, ft * P:(ft + 1) * P],
+                                        rhs=xcodes[g][:, src:src + width].bitcast(FP8X4),
+                                        rhs_scale=xscales[g][:, src:src + width],
+                                        start=True, stop=True)
+            w = n * P
+            pt = qk * 2 + a
+            o_e = rot.tile([P, E], F32, tag="o")
+            o_o = rot.tile([P, E], F32, tag="o")
+            o_tiles[(a, idx, 0)] = o_e
+            o_tiles[(a, idx, 1)] = o_o
+            t_e = terms.tile([P, E], F32, tag="te")
+            t_o = terms.tile([P, E], F32, tag="to")
+            nc.scalar.activation(out=t_e[:, :w], in_=bank_a[:, :w], func=ACT.Identity,
+                                 bias=bias_e[:, pt, pos:pos + 1], scale=cs[:, pos:pos + 1])
+            if GP_TAN:
+                nc.gpsimd.tensor_scalar(out=t_o[:, :w], in0=t_e[:, :w], scalar1=tan[:, pos:pos + 1],
+                                        scalar2=bias_t[:, pt, pos:pos + 1], op0=ALU.mult, op1=ALU.add)
+            else:
+                nc.scalar.activation(out=t_o[:, :w], in_=bank_a[:, :w], func=ACT.Identity,
+                                     bias=bias_o[:, pt, pos:pos + 1], scale=sn[:, pos:pos + 1])
+            nc.vector.scalar_tensor_tensor(out=o_e[:, :w], in0=bank_b[:, :w], scalar=nsn[:, pos:pos + 1],
+                                           in1=t_e[:, :w], op0=ALU.mult, op1=ALU.add)
+            nc.vector.scalar_tensor_tensor(out=o_o[:, :w], in0=bank_b[:, :w], scalar=cs[:, pos:pos + 1],
+                                           in1=t_o[:, :w], op0=ALU.mult, op1=ALU.add)
+
+        share = [0.0]
+
+        def token_bank(g, qk, ri, ci, o_tiles):
+            r0, nr, c0, ncol = grids[g]
+            at_zero = (r0 + ri == 0, c0 + ci == 0)
+            tok = ri * ncol + ci
+            stage = stage_pool.tile([P, E], F32, tag="stage")
+            bt = tp.tile([P, E], F32, tag="tp")
+            for a in range(2):
+                if at_zero[a]:
+                    nc.tensor.matmul_mx(out=bt[:, a * 256:(a + 1) * 256],
+                                        lhsT=xcodes[g][:, tok * P:(tok + 1) * P].bitcast(FP8X4),
+                                        lhsT_scale=xscales[g][:, tok * P:(tok + 1) * P],
+                                        rhs=wcodes[qk][:, a * 256:(a + 1) * 256].bitcast(FP8X4),
+                                        rhs_scale=wscales[qk][:, a * 256:(a + 1) * 256],
+                                        start=True, stop=True)
+                else:
+                    for e in range(2):
+                        if a == 0:
+                            src = o_tiles[(0, ri, e)][:, ci * P:(ci + 1) * P]
+                        else:
+                            src = o_tiles[(1, ci, e)][:, ri * P:(ri + 1) * P]
+                        blk = a * 2 + e
+                        nc.tensor.transpose(out=bt[:, blk * P:(blk + 1) * P], in_=src, identity=ident[:])
+            if at_zero[0] or at_zero[1]:
+                halves = stage[:].rearrange("p (h a j e) -> p a h j e", h=HEADS, a=2, j=NFREQ, e=2)
+                biases = btabs[qk][:].rearrange("p (h a j e) -> p a h j e", h=HEADS, a=2, j=NFREQ, e=2)
+                for a in range(2):
+                    view = bt[:, a * 256:(a + 1) * 256].rearrange("p (e h j) -> p h j e", e=2, h=HEADS, j=NFREQ)
+                    if at_zero[a]:
+                        nc.vector.tensor_tensor(out=halves[:, a], in0=view, in1=biases[:, a], op=ALU.add)
+                    else:
+                        nc.scalar.copy(out=halves[:, a], in_=view)
+            else:
+                dst = stage[:].rearrange("p (h a j e) -> p h a j e", h=HEADS, a=2, j=NFREQ, e=2)
+                view = bt[:].rearrange("p (a e h j) -> p h a j e", a=2, e=2, h=HEADS, j=NFREQ)
+                share[0] += SCALAR_SHARE
+                if share[0] >= 1.0:
+                    share[0] -= 1.0
+                    nc.scalar.copy(out=dst, in_=view)
+                else:
+                    nc.vector.tensor_copy(out=dst, in_=view)
+            nc.sync.dma_start(out=outs[qk][:, (r0 + ri) * GRID + c0 + ci, :], in_=stage[:])
+
+        def run_job(job):
+            if job[0] == "x":
+                x_bank(job[1], job[2], job[3], job[4], job[5])
+            else:
+                token_bank(job[1], job[2], job[3], job[4], job[5])
+
+        head = [x_open(0, 0)]
+        scale_table()
+        for job in head[0]:
+            run_job(job)
+        bias_prep()
+        w_prep(0)
+        for ri in range(1, grids[0][1]):
+            for job in x_open(0, ri):
+                run_job(job)
+            if ri == 1:
+                w_prep(1)
+
+        plan = []
+        per_grid = []
+        for g, (r0, nr, c0, ncol) in enumerate(grids):
+            before = len(plan)
+            for qk in range(2):
+                if g == 0 and qk == 0:
+                    order = [(0, ri) for ri in range(nr)] + [(1, ci) for ci in range(ncol)]
+                else:
+                    order = []
+                    for i in range(max(nr, ncol)):
+                        if i < ncol:
+                            order.append((1, i))
+                        if i < nr:
+                            order.append((0, i))
+                order = [(a, i) for (a, i) in order if (r0 + i if a == 0 else c0 + i) != 0]
+                plan.extend([(g, qk, a, i, n == 0) for n, (a, i) in enumerate(order)])
+            per_grid.append(len(plan) - before)
+        open_at = {}
+        start = 0
+        for g in range(len(grids) - 1):
+            nr_next = grids[g + 1][1]
+            for ri in range(nr_next):
+                open_at.setdefault(start + (ri * per_grid[g]) // (nr_next + 1), []).append((g + 1, ri))
+            start += per_grid[g]
+
+        fifo = []
+        waiting = []
+        o_now = {}
+        queued = set()
+        for u in range(len(plan) + LAG + 1):
+            for g, ri in open_at.get(u, []):
+                waiting.append((u + LAG, x_open(g, ri)))
+            if u < len(plan):
+                g, qk, a, idx, first = plan[u]
+                r0, nr, c0, ncol = grids[g]
+                if first:
+                    o_now = {}
+                    queued = set()
+                unit(g, qk, a, idx, o_now)
+                fresh = [(ri, ci) for ri in range(nr) for ci in range(ncol)
+                         if (ri, ci) not in queued
+                         and (r0 + ri == 0 or (0, ri, 0) in o_now)
+                         and (c0 + ci == 0 or (1, ci, 0) in o_now)]
+                for token in fresh:
+                    queued.add(token)
+                waiting.append((u + LAG, [("t", g, qk, ri, ci, o_now) for ri, ci in fresh]))
+            for ready, jobs in waiting:
+                if ready == u:
+                    fifo.extend(jobs)
+            last = u >= len(plan) + LAG
+            take = len(fifo) if last else min(len(fifo), MAX_JOBS if len(fifo) > 4 else 2)
+            for job in fifo[:take]:
+                run_job(job)
+            fifo = fifo[take:]

@@ -26,6 +26,7 @@ GP_TAN = True
 LAG = 2
 MANUAL_PE = False
 MAX_JOBS = 3
+X_SLACK = 2
 
 
 def tile_attention_pa_kernel(tc, x_bytes, x_scale, Wq, bq, Wk, bk, out_0, out_1):
@@ -39,12 +40,12 @@ def tile_attention_pa_kernel(tc, x_bytes, x_scale, Wq, bq, Wk, bk, out_0, out_1)
     with ExitStack() as ctx:
         const = ctx.enter_context(tc.tile_pool(name="const", bufs=1))
         wprep = ctx.enter_context(tc.tile_pool(name="wprep", bufs=2))
-        xstream = ctx.enter_context(tc.tile_pool(name="xstream", bufs=3))
+        xstream = ctx.enter_context(tc.tile_pool(name="xstream", bufs=6))
         terms = ctx.enter_context(tc.tile_pool(name="terms", bufs=4))
         rot = ctx.enter_context(tc.tile_pool(name="rot", bufs=32))
         stage_pool = ctx.enter_context(tc.tile_pool(name="stage", bufs=8))
-        mm = ctx.enter_context(tc.psum_pool(name="mm", bufs=2))
-        tp = ctx.enter_context(tc.psum_pool(name="tp", bufs=3))
+        mm = ctx.enter_context(tc.psum_pool(name="mm", bufs=8))
+        tp = mm
         if MANUAL_PE:
             ctx.enter_context(tc.manual_schedule(engines={mybir.EngineType.PE}))
 
@@ -150,7 +151,7 @@ def tile_attention_pa_kernel(tc, x_bytes, x_scale, Wq, bq, Wk, bk, out_0, out_1)
             bdst = bperm[:].rearrange("p (a e h j) -> p a e h j", a=2, e=2, h=HEADS, j=NFREQ)
             for a in range(2):
                 nc.gpsimd.tensor_copy(out=bdst[:, a], in_=bsrc[:, a])
-            bps = tp.tile([P, E], F32, tag="tp")
+            bps = tp.tile([P, E], F32, tag="bank")
             for blk in range(4):
                 nc.tensor.transpose(out=bps[:, blk * P:(blk + 1) * P], in_=bperm[:, blk * P:(blk + 1) * P],
                                     identity=ident[:])
@@ -197,43 +198,33 @@ def tile_attention_pa_kernel(tc, x_bytes, x_scale, Wq, bq, Wk, bk, out_0, out_1)
             wcodes.append(wc)
             wscales.append(ws)
 
-        def x_open(g, ri):
-            ncol = grids[g][3]
-            xs = xstream.tile([P, 4 * E], BF16, tag="xs", align_bytes=64)
-            if g == 0 and ri == 0:
-                for ci in range(ncol):
-                    nc.vector.tensor_tensor(out=xs[:, ci * E:(ci + 1) * E],
-                                            in0=xb[g][:, ri, ci * E:(ci + 1) * E].bitcast(FP8), in1=sc4[:, 0:E],
-                                            op=ALU.mult)
-            else:
-                nc.vector.tensor_tensor(out=xs[:, :ncol * E], in0=xb[g][:, ri, :].bitcast(FP8),
-                                        in1=sc4[:, :ncol * E], op=ALU.mult)
-            grp = xstream.tile([P, 4 * E], BF16, tag="grp", align_bytes=64)
-            return [("x", g, ri, first, xs, grp) for first in range(0, ncol, 2)]
+        def x_open(g, ri, first):
+            n2 = min(2, grids[g][3] - first)
+            xs = xstream.tile([P, 2 * E], BF16, tag="xs", align_bytes=64)
+            for lo, hi in ([(0, 1), (1, 2)] if (g == 0 and ri == 0 and first == 0) else [(0, n2)]):
+                nc.vector.tensor_tensor(out=xs[:, lo * E:hi * E],
+                                        in0=xb[g][:, ri, (first + lo) * E:(first + hi) * E].bitcast(FP8),
+                                        in1=sc4[:, :(hi - lo) * E], op=ALU.mult)
+            grp = xstream.tile([P, 2 * E], BF16, tag="grp", align_bytes=64)
+            return [("x", g, ri, first, xs, grp)]
 
         def x_bank(g, ri, first, xs, grp):
             ncol = grids[g][3]
             words = xs[:].bitcast(F32)
             gwords = grp[:].bitcast(F32)
             n2 = min(2, ncol - first)
-            xt = tp.tile([P, E], F32, tag="tp")
+            xt = tp.tile([P, E], F32, tag="bank")
             for s2 in range(n2):
-                ci = first + s2
                 for u in range(2):
                     nc.tensor.transpose(out=xt[:, (s2 * 2 + u) * P:(s2 * 2 + u + 1) * P],
-                                        in_=words[:, ci * 256 + u:(ci + 1) * 256:2], identity=ident[:])
+                                        in_=words[:, s2 * 256 + u:(s2 + 1) * 256:2], identity=ident[:])
             nc.scalar.copy(
-                out=gwords[:, first * 256:(first + n2) * 256].rearrange("p (s b u) -> p s b u", s=n2, u=2),
+                out=gwords[:, :n2 * 256].rearrange("p (s b u) -> p s b u", s=n2, u=2),
                 in_=xt[:, :n2 * 256].rearrange("p (s u b) -> p s b u", s=n2, u=2))
-            if first + n2 == ncol:
-                col = ri * ncol * P
-                off = 0
-                for width in ((2048,) if ncol == 4 else (1024, 512)):
-                    nc.vector.quantize_mx(out=xcodes[g][:, col:col + width // 4].bitcast(FP8X4),
-                                          scales=xscales[g][:, col:col + width // 4],
-                                          in_=grp[:, off:off + width])
-                    col += width // 4
-                    off += width
+            col = (ri * ncol + first) * P
+            nc.vector.quantize_mx(out=xcodes[g][:, col:col + n2 * P].bitcast(FP8X4),
+                                  scales=xscales[g][:, col:col + n2 * P],
+                                  in_=grp[:, :n2 * E])
 
         def unit(g, qk, a, idx, o_tiles):
             r0, nr, c0, ncol = grids[g]
@@ -246,8 +237,8 @@ def tile_attention_pa_kernel(tc, x_bytes, x_scale, Wq, bq, Wk, bk, out_0, out_1)
                 pos = c0 + idx
                 n = nr
                 chunks = [(ri * P, (ri * ncol + idx) * P, P) for ri in range(nr)]
-            bank_a = mm.tile([P, E], F32, tag="A")
-            bank_b = mm.tile([P, E], F32, tag="B", bufs=3)
+            bank_a = mm.tile([P, E], F32, tag="bank")
+            bank_b = mm.tile([P, E], F32, tag="bank")
             for e, bank in ((0, bank_a), (1, bank_b)):
                 ft = a * 2 + e
                 for dst, src, width in chunks:
@@ -285,7 +276,7 @@ def tile_attention_pa_kernel(tc, x_bytes, x_scale, Wq, bq, Wk, bk, out_0, out_1)
             at_zero = (r0 + ri == 0, c0 + ci == 0)
             tok = ri * ncol + ci
             stage = stage_pool.tile([P, E], F32, tag="stage")
-            bt = tp.tile([P, E], F32, tag="tp")
+            bt = tp.tile([P, E], F32, tag="bank")
             for a in range(2):
                 if at_zero[a]:
                     nc.tensor.matmul_mx(out=bt[:, a * 256:(a + 1) * 256],
@@ -328,15 +319,16 @@ def tile_attention_pa_kernel(tc, x_bytes, x_scale, Wq, bq, Wk, bk, out_0, out_1)
             else:
                 token_bank(job[1], job[2], job[3], job[4], job[5])
 
-        head = [x_open(0, 0)]
+        head = x_open(0, 0, 0)
         scale_table()
-        for job in head[0]:
+        for job in head + x_open(0, 0, 2):
             run_job(job)
         bias_prep()
         w_prep(0)
         for ri in range(1, grids[0][1]):
-            for job in x_open(0, ri):
-                run_job(job)
+            for first in range(0, grids[0][3], 2):
+                for job in x_open(0, ri, first):
+                    run_job(job)
             if ri == 1:
                 w_prep(1)
 
@@ -360,9 +352,9 @@ def tile_attention_pa_kernel(tc, x_bytes, x_scale, Wq, bq, Wk, bk, out_0, out_1)
         open_at = {}
         start = 0
         for g in range(len(grids) - 1):
-            nr_next = grids[g + 1][1]
-            for ri in range(nr_next):
-                open_at.setdefault(start + (ri * per_grid[g]) // (nr_next + 1), []).append((g + 1, ri))
+            pieces = [(g + 1, ri, first) for ri in range(grids[g + 1][1]) for first in range(0, grids[g + 1][3], 2)]
+            for n, piece in enumerate(pieces):
+                open_at.setdefault(start + (n * per_grid[g]) // (len(pieces) + X_SLACK), []).append(piece)
             start += per_grid[g]
 
         fifo = []
@@ -370,8 +362,8 @@ def tile_attention_pa_kernel(tc, x_bytes, x_scale, Wq, bq, Wk, bk, out_0, out_1)
         o_now = {}
         queued = set()
         for u in range(len(plan) + LAG + 1):
-            for g, ri in open_at.get(u, []):
-                waiting.append((u + LAG, x_open(g, ri)))
+            for g, ri, first in open_at.get(u, []):
+                waiting.append((u + LAG, x_open(g, ri, first)))
             if u < len(plan):
                 g, qk, a, idx, first = plan[u]
                 r0, nr, c0, ncol = grids[g]

@@ -20,7 +20,7 @@ HEADS = 8
 NFREQ = 16
 FLOPS = 2 * 128 * 49 * 512 * 1024
 
-SPLIT = ((0, 4), (4, 3))
+SPLIT = ((4, 3), (0, 4))
 SCALAR_SHARE = 1
 GP_TAN = True
 LAG = 2
@@ -55,7 +55,7 @@ def tile_attention_pa_kernel(tc, x_bytes, x_scale, Wq, bq, Wk, bk, out_0, out_1)
         brow = const.tile([P, E], BF16, name="brow")
         nc.vector.memset(brow[:], 0.0)
 
-        sc4 = const.tile([P, 4 * E], F32, name="sc4")
+        sc4 = const.tile([P, 2 * E], F32, name="sc4")
         nc.sync.dma_start(out=sc4[:, 0:E], in_=x_scale.rearrange("a b k -> (a b k)").partition_broadcast(P))
         xv = x_bytes.rearrange("b (r c) k -> b r (c k)", r=GRID, c=GRID)
         xb = []
@@ -86,7 +86,7 @@ def tile_attention_pa_kernel(tc, x_bytes, x_scale, Wq, bq, Wk, bk, out_0, out_1)
         load_x(0, (1, 2))
         nc.sync.dma_start(out=brow[0:1, :], in_=bq.rearrange("(o n) -> o n", o=1))
         nc.sync.dma_start(out=brow[1:2, :], in_=bk.rearrange("(o n) -> o n", o=1))
-        load_x(0, (2, 4))
+        load_x(0, (2, grids[0][1]))
         nc.sync.dma_start(out=wraws[1][:], in_=Wk.rearrange("(p t) n -> p t n", t=4))
         nc.sync.dma_start(out=btabs[0][:], in_=bq.partition_broadcast(P))
         nc.sync.dma_start(out=btabs[1][:], in_=bk.partition_broadcast(P))
@@ -180,7 +180,6 @@ def tile_attention_pa_kernel(tc, x_bytes, x_scale, Wq, bq, Wk, bk, out_0, out_1)
 
         def scale_table():
             nc.scalar.copy(out=sc4[:, E:2 * E], in_=sc4[:, 0:E])
-            nc.scalar.copy(out=sc4[:, 2 * E:4 * E], in_=sc4[:, 0:2 * E])
 
         wcodes = []
         wscales = []
@@ -191,7 +190,11 @@ def tile_attention_pa_kernel(tc, x_bytes, x_scale, Wq, bq, Wk, bk, out_0, out_1)
             dst = wgrp[:].rearrange("p (a e h j) t -> p a e h j t", a=2, e=2, h=HEADS, j=NFREQ)
             for a in range(2):
                 for e in range(2):
-                    nc.scalar.copy(out=dst[:, a, e], in_=src[:, a, e])
+                    if qk == 0:
+                        nc.scalar.copy(out=dst[:, a, e], in_=src[:, a, e])
+                    else:
+                        nc.gpsimd.tensor_scalar(out=dst[:, a, e], in0=src[:, a, e], scalar1=1.0, scalar2=0.0,
+                                                op0=ALU.mult, op1=ALU.add)
             wc = const.tile([P, E], U32, name="wc%d" % qk, align_bytes=64)
             ws = const.tile([P, E], U8, name="ws%d" % qk, align_bytes=64)
             nc.vector.quantize_mx(out=wc[:].bitcast(FP8X4), scales=ws[:], in_=wgrp[:].rearrange("p c t -> p (c t)"))

@@ -150,7 +150,7 @@ def tile_attention_pa_kernel(tc, x_bytes, x_scale, Wq, bq, Wk, bk, out_0, out_1)
             bsrc = brow[:].rearrange("p (h a j e) -> p a e h j", h=HEADS, a=2, j=NFREQ, e=2)
             bdst = bperm[:].rearrange("p (a e h j) -> p a e h j", a=2, e=2, h=HEADS, j=NFREQ)
             for a in range(2):
-                nc.gpsimd.tensor_copy(out=bdst[:, a], in_=bsrc[:, a])
+                nc.gpsimd.tensor_scalar(out=bdst[:, a], in0=bsrc[:, a], scalar1=1.0, scalar2=0.0, op0=ALU.mult, op1=ALU.add)
             bps = tp.tile([P, E], F32, tag="bank")
             for blk in range(4):
                 nc.tensor.transpose(out=bps[:, blk * P:(blk + 1) * P], in_=bperm[:, blk * P:(blk + 1) * P],
@@ -164,19 +164,10 @@ def tile_attention_pa_kernel(tc, x_bytes, x_scale, Wq, bq, Wk, bk, out_0, out_1)
             sn_b = sn[:].unsqueeze(1).to_broadcast(shape)
             m1 = const.tile(shape, F32, name="m1")
             m2 = const.tile(shape, F32, name="m2")
-            m3 = const.tile(shape, F32, name="m3")
-            m4 = const.tile(shape, F32, name="m4")
             nc.gpsimd.tensor_tensor(out=m1[:], in0=cs_b, in1=b_a, op=ALU.mult)
             nc.gpsimd.tensor_tensor(out=m2[:], in0=sn_b, in1=b_b, op=ALU.mult)
-            nc.gpsimd.tensor_tensor(out=m3[:], in0=sn_b, in1=b_a, op=ALU.mult)
-            nc.gpsimd.tensor_tensor(out=m4[:], in0=cs_b, in1=b_b, op=ALU.mult)
             nc.gpsimd.tensor_tensor(out=bias_e[:], in0=m1[:], in1=m2[:], op=ALU.subtract)
-            nc.gpsimd.tensor_tensor(out=bias_o[:], in0=m3[:], in1=m4[:], op=ALU.add)
-            if GP_TAN:
-                m5 = const.tile(shape, F32, name="m5")
-                nc.gpsimd.tensor_tensor(out=m5[:], in0=tan[:].unsqueeze(1).to_broadcast(shape), in1=bias_e[:],
-                                        op=ALU.mult)
-                nc.gpsimd.tensor_tensor(out=bias_t[:], in0=bias_o[:], in1=m5[:], op=ALU.subtract)
+            nc.gpsimd.tensor_tensor(out=bias_t[:], in0=rcs[:].unsqueeze(1).to_broadcast(shape), in1=b_b, op=ALU.mult)
 
         def scale_table():
             nc.scalar.copy(out=sc4[:, E:2 * E], in_=sc4[:, 0:E])

from contextlib import ExitStack

import concourse.mybir as mybir
from concourse.masks import make_identity

F32 = mybir.dt.float32
BF16 = mybir.dt.bfloat16
U32 = mybir.dt.uint32
U8 = mybir.dt.uint8
I32 = mybir.dt.int32
FP8 = mybir.dt.float8_e4m3fn
FP8X4 = mybir.dt.float8_e4m3fn_x4
ALU = mybir.AluOpType
ACT = mybir.ActivationFunctionType

P = 128
GRID = 7
E = 512
HEADS = 8
NFREQ = 16
FLOPS = 2 * 128 * 49 * 512 * 1024

SPLIT = ((4, 3), (0, 4))
SCALAR_SHARE = 1
GP_TAN = True
LAG = 2
MANUAL_PE = False
MAX_JOBS = 3
X_SLACK = 2


def tile_attention_pa_kernel(tc, x_bytes, x_scale, Wq, bq, Wk, bk, out_0, out_1):
    nc = tc.nc
    grids = [(r0, nr, c0, ncol) for (r0, nr) in SPLIT for (c0, ncol) in SPLIT]
    outs = (
        out_0.rearrange("b s h d -> b s (h d)"),
        out_1.rearrange("b s h d -> b s (h d)"),
    )

    with ExitStack() as ctx:
        const = ctx.enter_context(tc.tile_pool(name="const", bufs=1))
        wprep = ctx.enter_context(tc.tile_pool(name="wprep", bufs=2))
        xstream = ctx.enter_context(tc.tile_pool(name="xstream", bufs=6))
        terms = ctx.enter_context(tc.tile_pool(name="terms", bufs=4))
        rot = ctx.enter_context(tc.tile_pool(name="rot", bufs=32))
        stage_pool = ctx.enter_context(tc.tile_pool(name="stage", bufs=8))
        mm = ctx.enter_context(tc.psum_pool(name="mm", bufs=8))
        tp = mm
        if MANUAL_PE:
            ctx.enter_context(tc.manual_schedule(engines={mybir.EngineType.PE}))

        ident = const.tile([P, P], F32, name="ident")
        nc.vector.memset(ident[:], 0.0)
        make_identity(nc, ident[:], nomemset=True)
        brow = const.tile([P, E], BF16, name="brow")
        nc.vector.memset(brow[:], 0.0)

        sc4 = const.tile([P, 2 * E], F32, name="sc4")
        nc.sync.dma_start(out=sc4[:, 0:E], in_=x_scale.rearrange("a b k -> (a b k)").partition_broadcast(P))
        xv = x_bytes.rearrange("b (r c) k -> b r (c k)", r=GRID, c=GRID)
        xb = []
        xcodes = []
        xscales = []
        for g, (r0, nr, c0, ncol) in enumerate(grids):
            xb_g = const.tile([P, nr, ncol * E], U8, name="xb%d" % g)
            xc_g = const.tile([P, nr * ncol * P], U32, name="xc%d" % g, align_bytes=64)
            xs_g = const.tile([P, nr * ncol * P], U8, name="xs%d" % g, align_bytes=64)
            xb.append(xb_g)
            xcodes.append(xc_g)
            xscales.append(xs_g)
        wraws = []
        btabs = []
        for qk in range(2):
            wraw = wprep.tile([P, 4, E], BF16, tag="wraw")
            wraws.append(wraw)
            btab = const.tile([P, E], BF16, name="btab%d" % qk)
            btabs.append(btab)

        def load_x(g, rows):
            r0, nr, c0, ncol = grids[g]
            nc.sync.dma_start(out=xb[g][:, rows[0]:rows[1], :],
                              in_=xv[:, r0 + rows[0]:r0 + rows[1], c0 * E:(c0 + ncol) * E])

        load_x(0, (0, 1))
        nc.sync.dma_start(out=wraws[0][:], in_=Wq.rearrange("(p t) n -> p t n", t=4))
        load_x(0, (1, 2))
        nc.sync.dma_start(out=brow[0:1, :], in_=bq.rearrange("(o n) -> o n", o=1))
        nc.sync.dma_start(out=brow[1:2, :], in_=bk.rearrange("(o n) -> o n", o=1))
        load_x(0, (2, grids[0][1]))
        nc.sync.dma_start(out=wraws[1][:], in_=Wk.rearrange("(p t) n -> p t n", t=4))
        nc.sync.dma_start(out=btabs[0][:], in_=bq.partition_broadcast(P))
        nc.sync.dma_start(out=btabs[1][:], in_=bk.partition_broadcast(P))
        for g in range(1, len(grids)):
            load_x(g, (0, grids[g][1]))

        pidx = const.tile([P, 1], I32, name="pidx")
        nc.gpsimd.iota(pidx[:], pattern=[[0, 1]], base=0, channel_multiplier=1)
        posi = const.tile([P, GRID], I32, name="posi")
        nc.gpsimd.iota(posi[:], pattern=[[1, GRID]], base=0, channel_multiplier=0)
        bits = const.tile([P, 4], I32, name="bits")
        fac = const.tile([P, 4], F32, name="fac")
        for i in range(4):
            nc.vector.tensor_scalar(out=bits[:, i:i + 1], in0=pidx[:], scalar1=i, scalar2=1,
                                    op0=ALU.logical_shift_right, op1=ALU.bitwise_and)
        for i in range(4):
            g_i = 100.0 ** (-(2.0 ** i) / 16.0)
            nc.vector.tensor_scalar(out=fac[:, i:i + 1], in0=bits[:, i:i + 1], scalar1=g_i - 1.0, scalar2=1.0,
                                    op0=ALU.mult, op1=ALU.add)
        f01 = const.tile([P, 1], F32, name="f01")
        f23 = const.tile([P, 1], F32, name="f23")
        freq = const.tile([P, 1], F32, name="freq")
        nc.vector.tensor_tensor(out=f01[:], in0=fac[:, 0:1], in1=fac[:, 1:2], op=ALU.mult)
        nc.vector.tensor_tensor(out=f23[:], in0=fac[:, 2:3], in1=fac[:, 3:4], op=ALU.mult)
        nc.vector.tensor_tensor(out=freq[:], in0=f01[:], in1=f23[:], op=ALU.mult)
        theta = const.tile([P, GRID], F32, name="theta")
        nc.vector.tensor_scalar(out=theta[:], in0=posi[:], scalar1=freq[:, 0:1], scalar2=None, op0=ALU.mult)
        s8 = const.tile([P, GRID], F32, name="s8")
        s4 = const.tile([P, GRID], F32, name="s4")
        nc.scalar.activation(out=s8[:], in_=theta[:], func=ACT.Sin, scale=0.125)
        nc.scalar.activation(out=s4[:], in_=theta[:], func=ACT.Sin, scale=0.25)

        def one_minus_twice_square(name, s_ap):
            sq = const.tile([P, GRID], F32, name=name + "_sq")
            c_t = const.tile([P, GRID], F32, name=name)
            nc.vector.tensor_tensor(out=sq[:], in0=s_ap, in1=s_ap, op=ALU.mult)
            nc.vector.tensor_scalar(out=c_t[:], in0=sq[:], scalar1=-2.0, scalar2=1.0, op0=ALU.mult, op1=ALU.add)
            return c_t

        c4 = one_minus_twice_square("c4", s8[:])
        s2 = const.tile([P, GRID], F32, name="s2")
        nc.vector.scalar_tensor_tensor(out=s2[:], in0=s4[:], scalar=2.0, in1=c4[:], op0=ALU.mult, op1=ALU.mult)
        c2 = one_minus_twice_square("c2", s4[:])
        sn = const.tile([P, GRID], F32, name="sn")
        nc.vector.scalar_tensor_tensor(out=sn[:], in0=s2[:], scalar=2.0, in1=c2[:], op0=ALU.mult, op1=ALU.mult)
        cs = one_minus_twice_square("cs", s2[:])
        nsn = const.tile([P, GRID], F32, name="nsn")
        nc.vector.tensor_scalar(out=nsn[:], in0=sn[:], scalar1=-1.0, scalar2=None, op0=ALU.mult)
        tan = const.tile([P, GRID], F32, name="tan")
        if GP_TAN:
            rcs = const.tile([P, GRID], F32, name="rcs")
            nc.vector.reciprocal(out=rcs[:], in_=cs[:])
            nc.vector.tensor_tensor(out=tan[:], in0=sn[:], in1=rcs[:], op=ALU.mult)

        bias_e = const.tile([P, 4, GRID], F32, name="bias_e")
        bias_o = const.tile([P, 4, GRID], F32, name="bias_o")
        bias_t = const.tile([P, 4, GRID], F32, name="bias_t")

        def bias_prep():
            bperm = const.tile([P, E], F32, name="bperm")
            bsrc = brow[:].rearrange("p (h a j e) -> p a e h j", h=HEADS, a=2, j=NFREQ, e=2)
            bdst = bperm[:].rearrange("p (a e h j) -> p a e h j", a=2, e=2, h=HEADS, j=NFREQ)
            for a in range(2):
                nc.gpsimd.tensor_scalar(out=bdst[:, a], in0=bsrc[:, a], scalar1=1.0, scalar2=0.0, op0=ALU.mult, op1=ALU.add)
            bps = tp.tile([P, E], F32, tag="bank")
            for blk in range(4):
                nc.tensor.transpose(out=bps[:, blk * P:(blk + 1) * P], in_=bperm[:, blk * P:(blk + 1) * P],
                                    identity=ident[:])
            bc = const.tile([P, 2, 2, 2], F32, name="bc")
            nc.scalar.copy(out=bc[:], in_=bps[:].rearrange("p (a e n) -> p e n a", a=2, e=2)[:, :, 0:2, :])
            shape = [P, 4, GRID]
            b_a = bc[:, 0].rearrange("p q a -> p (q a)").unsqueeze(2).to_broadcast(shape)
            b_b = bc[:, 1].rearrange("p q a -> p (q a)").unsqueeze(2).to_broadcast(shape)
            cs_b = cs[:].unsqueeze(1).to_broadcast(shape)
            sn_b = sn[:].unsqueeze(1).to_broadcast(shape)
            m1 = const.tile(shape, F32, name="m1")
            m2 = const.tile(shape, F32, name="m2")
            nc.gpsimd.tensor_tensor(out=m1[:], in0=cs_b, in1=b_a, op=ALU.mult)
            nc.gpsimd.tensor_tensor(out=m2[:], in0=sn_b, in1=b_b, op=ALU.mult)
            nc.gpsimd.tensor_tensor(out=bias_e[:], in0=m1[:], in1=m2[:], op=ALU.subtract)
            nc.gpsimd.tensor_tensor(out=bias_t[:], in0=rcs[:].unsqueeze(1).to_broadcast(shape), in1=b_b, op=ALU.mult)

        def scale_table():
            nc.scalar.copy(out=sc4[:, E:2 * E], in_=sc4[:, 0:E])

        wcodes = []
        wscales = []

        def w_prep(qk):
            wgrp = wprep.tile([P, E, 4], BF16, tag="wgrp", align_bytes=64)
            src = wraws[qk][:].rearrange("p t (h a j e) -> p a e h j t", h=HEADS, a=2, j=NFREQ, e=2)
            dst = wgrp[:].rearrange("p (a e h j) t -> p a e h j t", a=2, e=2, h=HEADS, j=NFREQ)
            for a in range(2):
                for e in range(2):
                    if qk == 0:
                        nc.scalar.copy(out=dst[:, a, e], in_=src[:, a, e])
                    else:
                        nc.gpsimd.tensor_scalar(out=dst[:, a, e], in0=src[:, a, e], scalar1=1.0, scalar2=0.0,
                                                op0=ALU.mult, op1=ALU.add)
            wc = const.tile([P, E], U32, name="wc%d" % qk, align_bytes=64)
            ws = const.tile([P, E], U8, name="ws%d" % qk, align_bytes=64)
            nc.vector.quantize_mx(out=wc[:].bitcast(FP8X4), scales=ws[:], in_=wgrp[:].rearrange("p c t -> p (c t)"))
            wcodes.append(wc)
            wscales.append(ws)

        def x_open(g, ri, first):
            n2 = min(2, grids[g][3] - first)
            xs = xstream.tile([P, 2 * E], BF16, tag="xs", align_bytes=64)
            for lo, hi in ([(0, 1), (1, 2)] if (g == 0 and ri == 0 and first == 0) else [(0, n2)]):
                nc.vector.tensor_tensor(out=xs[:, lo * E:hi * E],
                                        in0=xb[g][:, ri, (first + lo) * E:(first + hi) * E].bitcast(FP8),
                                        in1=sc4[:, :(hi - lo) * E], op=ALU.mult)
            grp = xstream.tile([P, 2 * E], BF16, tag="grp", align_bytes=64)
            return [("x", g, ri, first, xs, grp)]

        def x_bank(g, ri, first, xs, grp):
            ncol = grids[g][3]
            words = xs[:].bitcast(F32)
            gwords = grp[:].bitcast(F32)
            n2 = min(2, ncol - first)
            xt = tp.tile([P, E], F32, tag="bank")
            for s2 in range(n2):
                for u in range(2):
                    nc.tensor.transpose(out=xt[:, (s2 * 2 + u) * P:(s2 * 2 + u + 1) * P],
                                        in_=words[:, s2 * 256 + u:(s2 + 1) * 256:2], identity=ident[:])
            nc.scalar.copy(
                out=gwords[:, :n2 * 256].rearrange("p (s b u) -> p s b u", s=n2, u=2),
                in_=xt[:, :n2 * 256].rearrange("p (s u b) -> p s b u", s=n2, u=2))
            col = (ri * ncol + first) * P
            nc.vector.quantize_mx(out=xcodes[g][:, col:col + n2 * P].bitcast(FP8X4),
                                  scales=xscales[g][:, col:col + n2 * P],
                                  in_=grp[:, :n2 * E])

        def unit(g, qk, a, idx, o_tiles):
            r0, nr, c0, ncol = grids[g]
            if a == 0:
                pos = r0 + idx
                n = ncol
                base = idx * ncol * P
                chunks = [(0, base, 512)] if ncol == 4 else [(0, base, 256), (256, base + 256, 128)]
            else:
                pos = c0 + idx
                n = nr
                chunks = [(ri * P, (ri * ncol + idx) * P, P) for ri in range(nr)]
            bank_a = mm.tile([P, E], F32, tag="bank")
            bank_b = mm.tile([P, E], F32, tag="bank")
            for e, bank in ((0, bank_a), (1, bank_b)):
                ft = a * 2 + e
                for dst, src, width in chunks:
                    nc.tensor.matmul_mx(out=bank[:, dst:dst + width],
                                        lhsT=wcodes[qk][:, ft * P:(ft + 1) * P].bitcast(FP8X4),
                                        lhsT_scale=wscales[qk][:, ft * P:(ft + 1) * P],
                                        rhs=xcodes[g][:, src:src + width].bitcast(FP8X4),
                                        rhs_scale=xscales[g][:, src:src + width],
                                        start=True, stop=True)
            w = n * P
            pt = qk * 2 + a
            o_e = rot.tile([P, E], F32, tag="o")
            o_o = rot.tile([P, E], F32, tag="o")
            o_tiles[(a, idx, 0)] = o_e
            o_tiles[(a, idx, 1)] = o_o
            t_e = terms.tile([P, E], F32, tag="te")
            t_o = terms.tile([P, E], F32, tag="to")
            nc.scalar.activation(out=t_e[:, :w], in_=bank_a[:, :w], func=ACT.Identity,
                                 bias=bias_e[:, pt, pos:pos + 1], scale=cs[:, pos:pos + 1])
            if GP_TAN:
                nc.gpsimd.tensor_scalar(out=t_o[:, :w], in0=t_e[:, :w], scalar1=tan[:, pos:pos + 1],
                                        scalar2=bias_t[:, pt, pos:pos + 1], op0=ALU.mult, op1=ALU.add)
            else:
                nc.scalar.activation(out=t_o[:, :w], in_=bank_a[:, :w], func=ACT.Identity,
                                     bias=bias_o[:, pt, pos:pos + 1], scale=sn[:, pos:pos + 1])
            nc.vector.scalar_tensor_tensor(out=o_e[:, :w], in0=bank_b[:, :w], scalar=nsn[:, pos:pos + 1],
                                           in1=t_e[:, :w], op0=ALU.mult, op1=ALU.add)
            nc.vector.scalar_tensor_tensor(out=o_o[:, :w], in0=bank_b[:, :w], scalar=cs[:, pos:pos + 1],
                                           in1=t_o[:, :w], op0=ALU.mult, op1=ALU.add)

        share = [0.0]

        def token_bank(g, qk, ri, ci, o_tiles):
            r0, nr, c0, ncol = grids[g]
            at_zero = (r0 + ri == 0, c0 + ci == 0)
            tok = ri * ncol + ci
            stage = stage_pool.tile([P, E], F32, tag="stage")
            bt = tp.tile([P, E], F32, tag="bank")
            for a in range(2):
                if at_zero[a]:
                    nc.tensor.matmul_mx(out=bt[:, a * 256:(a + 1) * 256],
                                        lhsT=xcodes[g][:, tok * P:(tok + 1) * P].bitcast(FP8X4),
                                        lhsT_scale=xscales[g][:, tok * P:(tok + 1) * P],
                                        rhs=wcodes[qk][:, a * 256:(a + 1) * 256].bitcast(FP8X4),
                                        rhs_scale=wscales[qk][:, a * 256:(a + 1) * 256],
                                        start=True, stop=True)
                else:
                    for e in range(2):
                        if a == 0:
                            src = o_tiles[(0, ri, e)][:, ci * P:(ci + 1) * P]
                        else:
                            src = o_tiles[(1, ci, e)][:, ri * P:(ri + 1) * P]
                        blk = a * 2 + e
                        nc.tensor.transpose(out=bt[:, blk * P:(blk + 1) * P], in_=src, identity=ident[:])
            if at_zero[0] or at_zero[1]:
                halves = stage[:].rearrange("p (h a j e) -> p a h j e", h=HEADS, a=2, j=NFREQ, e=2)
                biases = btabs[qk][:].rearrange("p (h a j e) -> p a h j e", h=HEADS, a=2, j=NFREQ, e=2)
                for a in range(2):
                    view = bt[:, a * 256:(a + 1) * 256].rearrange("p (e h j) -> p h j e", e=2, h=HEADS, j=NFREQ)
                    if at_zero[a]:
                        nc.vector.tensor_tensor(out=halves[:, a], in0=view, in1=biases[:, a], op=ALU.add)
                    else:
                        nc.scalar.copy(out=halves[:, a], in_=view)
            else:
                dst = stage[:].rearrange("p (h a j e) -> p h a j e", h=HEADS, a=2, j=NFREQ, e=2)
                view = bt[:].rearrange("p (a e h j) -> p h a j e", a=2, e=2, h=HEADS, j=NFREQ)
                share[0] += SCALAR_SHARE
                if share[0] >= 1.0:
                    share[0] -= 1.0
                    nc.scalar.copy(out=dst, in_=view)
                else:
                    nc.vector.tensor_copy(out=dst, in_=view)
            nc.sync.dma_start(out=outs[qk][:, (r0 + ri) * GRID + c0 + ci, :], in_=stage[:])

        def run_job(job):
            if job[0] == "x":
                x_bank(job[1], job[2], job[3], job[4], job[5])
            else:
                token_bank(job[1], job[2], job[3], job[4], job[5])

        head = x_open(0, 0, 0)
        scale_table()
        for job in head + x_open(0, 0, 2):
            run_job(job)
        bias_prep()
        w_prep(0)
        for ri in range(1, grids[0][1]):
            for first in range(0, grids[0][3], 2):
                for job in x_open(0, ri, first):
                    run_job(job)
            if ri == 1:
                w_prep(1)

        plan = []
        per_grid = []
        for g, (r0, nr, c0, ncol) in enumerate(grids):
            before = len(plan)
            for qk in range(2):
                if g == 0 and qk == 0:
                    order = [(0, ri) for ri in range(nr)] + [(1, ci) for ci in range(ncol)]
                else:
                    order = []
                    for i in range(max(nr, ncol)):
                        if i < ncol:
                            order.append((1, i))
                        if i < nr:
                            order.append((0, i))
                order = [(a, i) for (a, i) in order if (r0 + i if a == 0 else c0 + i) != 0]
                plan.extend([(g, qk, a, i, n == 0) for n, (a, i) in enumerate(order)])
            per_grid.append(len(plan) - before)
        open_at = {}
        start = 0
        for g in range(len(grids) - 1):
            pieces = [(g + 1, ri, first) for ri in range(grids[g + 1][1]) for first in range(0, grids[g + 1][3], 2)]
            for n, piece in enumerate(pieces):
                open_at.setdefault(start + (n * per_grid[g]) // (len(pieces) + X_SLACK), []).append(piece)
            start += per_grid[g]

        fifo = []
        waiting = []
        o_now = {}
        queued = set()
        for u in range(len(plan) + LAG + 1):
            for g, ri, first in open_at.get(u, []):
                waiting.append((u + LAG, x_open(g, ri, first)))
            if u < len(plan):
                g, qk, a, idx, first = plan[u]
                r0, nr, c0, ncol = grids[g]
                if first:
                    o_now = {}
                    queued = set()
                unit(g, qk, a, idx, o_now)
                fresh = [(ri, ci) for ri in range(nr) for ci in range(ncol)
                         if (ri, ci) not in queued
                         and (r0 + ri == 0 or (0, ri, 0) in o_now)
                         and (c0 + ci == 0 or (1, ci, 0) in o_now)]
                for token in fresh:
                    queued.add(token)
                waiting.append((u + LAG, [("t", g, qk, ri, ci, o_now) for ri, ci in fresh]))
            for ready, jobs in waiting:
                if ready == u:
                    fifo.extend(jobs)
            last = u >= len(plan) + LAG
            take = len(fifo) if last else min(len(fifo), MAX_JOBS if len(fifo) > 4 else 2)
            for job in fifo[:take]:
                run_job(job)
            fifo = fifo[take:]
